import numpy as np
import ml_dtypes


def mxq(x, axis, fmt="e4m3"):
    dtype, down = {"e4m3": (ml_dtypes.float8_e4m3fn, 7), "e5m2": (ml_dtypes.float8_e5m2, 14)}[fmt]
    v = np.moveaxis(np.asarray(x, np.float32).astype(ml_dtypes.bfloat16).astype(np.float64), axis, -1)
    blocks = v.reshape(v.shape[:-1] + (-1, 32))
    amax = np.abs(blocks).max(-1, keepdims=True)
    byte = np.maximum(np.where(amax > 0, np.frexp(amax)[1] - 1 + 127, 0) - down, 1)
    scale = np.exp2(byte - 127.0)
    codes = (blocks / scale).astype(np.float32).astype(dtype).astype(np.float64)
    return np.moveaxis((codes * scale).reshape(v.shape), -1, axis)


WIDE = False


def mx_kscale(k):
    if not WIDE:
        return np.ones(k)
    levels = np.array([10, -10, 5, -5, 0])
    if k % 512:
        return np.exp2(np.random.permutation(np.resize(levels, k // 32))).repeat(32)
    a = np.empty((k // 512, 16))
    for p in range(k // 512):
        a[p, :8] = np.random.permutation(np.resize(levels, 8))
        for g in range(8):
            far = levels[np.abs(levels - a[p, g]) >= 10]
            a[p, g + 8] = far[np.random.randint(len(far))]
    return np.exp2(a.ravel()).repeat(32)


BF16 = ml_dtypes.bfloat16


def bf(x):
    return np.asarray(x, np.float32).astype(BF16)


def f64(x):
    return np.asarray(x).astype(np.float64)


B, D, DO, H, T, P = 8192, 512, 1024, 256, 8, 2


def setup_inputs():
    s = mx_kscale(D)
    return {"transformed": bf(np.random.standard_normal((B, D)) * 1.2 * s),
            "coeff": bf(np.random.standard_normal((B, P)) * 0.45),
            "task_mats": bf(np.random.standard_normal((P, D, D)) / np.sqrt(D) / s[None, :, None] * s[None, None, :])}


def reference(transformed, coeff, task_mats):
    x, c, m = f64(transformed), f64(coeff), f64(task_mats)
    for j in range(P):
        x = x + c[:, j:j + 1] * (mxq(x, 1, "e4m3") @ mxq(m[j], 0, "e4m3"))
    return x

@@ -1,0 +1,248 @@
+from contextlib import ExitStack
+
+import concourse.mybir as mybir
+from concourse.masks import make_identity
+
+F32 = mybir.dt.float32
+BF16 = mybir.dt.bfloat16
+U32 = mybir.dt.uint32
+U8 = mybir.dt.uint8
+FP8X4 = mybir.dt.float8_e4m3fn_x4
+MULT = mybir.AluOpType.mult
+ADD = mybir.AluOpType.add
+COPY = mybir.ActivationFunctionType.Copy
+
+P = 128
+B = 8192
+D = 512
+NT = B // P
+NP = NT // 2
+FLOPS = 2 * 2 * B * D * D
+
+CHUNKS = [2, 2, 4, 8, 8, 8, 8, 8, 8, 8]
+W0_SPLIT = 384
+
+
+def tile_precomputedmetanet_pa_t_kernel(tc, transformed, coeff, task_mats, out):
+    nc = tc.nc
+    x_dram = transformed.rearrange("(p i) d -> p (i d)", i=NT)
+    o_dram = out.rearrange("(p i) d -> p (i d)", i=NT)
+    c_dram = coeff.rearrange("(p i) c -> p (i c)", i=NT)
+
+    with ExitStack() as ctx:
+        const = ctx.enter_context(tc.tile_pool(name="const", bufs=1))
+        gpool = ctx.enter_context(tc.tile_pool(name="gpool", bufs=3))
+        qpool = ctx.enter_context(tc.tile_pool(name="qpool", bufs=3))
+        x1pool = ctx.enter_context(tc.tile_pool(name="x1pool", bufs=6))
+        opool = ctx.enter_context(tc.tile_pool(name="opool", bufs=6))
+        czpool = ctx.enter_context(tc.tile_pool(name="czpool", bufs=3))
+        ps_x = ctx.enter_context(tc.psum_pool(name="ps_x", bufs=2))
+        ps_t = ctx.enter_context(tc.psum_pool(name="ps_t", bufs=2))
+        ps_y = ctx.enter_context(tc.psum_pool(name="ps_y", bufs=2))
+        ps_z = ctx.enter_context(tc.psum_pool(name="ps_z", bufs=2))
+        ctx.enter_context(tc.manual_schedule())
+
+        ident = const.tile([P, P], F32, name="ident")
+        make_identity(nc, ident[:])
+
+        w0r = const.tile([P, 4, D], BF16, name="w0r")
+        nc.sync.dma_start(out=w0r[:], in_=task_mats[0].rearrange("(p t) n -> p t n", t=4))
+        xs = []
+        where = {}
+        start = 0
+        w1r = const.tile([P, 4, D], BF16, name="w1r")
+        c_bf = const.tile([P, 2 * NT], BF16, name="c_bf")
+        for c, n in enumerate(CHUNKS):
+            xc = const.tile([P, n * D], BF16, name="x%d" % c)
+            nc.sync.dma_start(out=xc[:], in_=x_dram[:, start * D : (start + n) * D])
+            xs.append(xc)
+            for k in range(n):
+                where[start + k] = (c, k)
+            start += n
+            if c == 0:
+                nc.sync.dma_start(out=c_bf[:], in_=c_dram)
+            if c == 1:
+                nc.sync.dma_start(out=w1r[:], in_=task_mats[1].rearrange("(p t) n -> p t n", t=4))
+        assert start == NT
+
+        def x_bf(i):
+            c, k = where[i]
+            return xs[c][:, k * D : (k + 1) * D]
+
+        def x_words(i, u):
+            c, k = where[i]
+            lo = k * (D // 2)
+            return xs[c][:].bitcast(F32)[:, lo + u : lo + 2 * P : 2]
+
+        w0g = const.tile([P, D, 4], BF16, name="w0g", align_bytes=64)
+        w0c = const.tile([P, D], U32, name="w0c", align_bytes=64)
+        w0s = const.tile([P, D], U8, name="w0s", align_bytes=64)
+        w1g = const.tile([P, D, 4], BF16, name="w1g", align_bytes=64)
+        w1c = const.tile([P, D], U32, name="w1c", align_bytes=64)
+        w1s = const.tile([P, D], U8, name="w1s", align_bytes=64)
+        c32 = const.tile([P, 2 * NT], F32, name="c32")
+
+        nc.vector.tensor_copy(
+            out=w0g[:, 0:W0_SPLIT, :].rearrange("p (c i) t -> p c t i", i=4),
+            in_=w0r[:, :, 0:W0_SPLIT].rearrange("p t (c i) -> p c t i", i=4),
+        )
+        nc.scalar.copy(
+            out=w0g[:, W0_SPLIT:D, :].rearrange("p (c i) t -> p c t i", i=4),
+            in_=w0r[:, :, W0_SPLIT:D].rearrange("p t (c i) -> p c t i", i=4),
+        )
+        nc.vector.tensor_copy(out=c32[:], in_=c_bf[:])
+        nc.vector.quantize_mx(
+            out=w0c[:].bitcast(FP8X4), scales=w0s[:], in_=w0g[:].rearrange("p n t -> p (n t)")
+        )
+
+        TPX = {}
+        GX = {}
+        QX = {}
+        Y = {}
+        X1 = {}
+        T1 = {}
+        G1 = {}
+        Q1 = {}
+        Z = {}
+        O = {}
+        CZ = {}
+
+        def tx(g):
+            t = ps_x.tile([P, 2, 2, P], F32, name="tpx", tag="tpx")
+            for j in range(2):
+                for u in range(2):
+                    nc.tensor.transpose(t[:, j, u, :], x_words(2 * g + j, u), ident[:])
+            TPX[g] = t
+
+        def ex(g):
+            gx = gpool.tile([P, 8 * P], BF16, name="gx", tag="gx", align_bytes=64)
+            nc.scalar.copy(
+                out=gx[:].bitcast(F32).rearrange("p (j k u) -> p j k u", j=2, u=2),
+                in_=TPX[g][:].rearrange("p j u k -> p j k u"),
+            )
+            GX[g] = gx
+
+        def quant(src, tagc, tags):
+            cw = qpool.tile([P, 2 * P], U32, name=tagc, tag=tagc, align_bytes=64)
+            sc = qpool.tile([P, 2 * P], U8, name=tags, tag=tags, align_bytes=64)
+            nc.vector.quantize_mx(out=cw[:].bitcast(FP8X4), scales=sc[:], in_=src[:])
+            return (cw, sc)
+
+        def mm(pool, tag, q, wc, ws):
+            res = {}
+            cw, sc = q
+            for j in (1, 0) if tag == "z" else (0, 1):
+                acc = pool.tile([P, D], F32, name=tag, tag=tag)
+                nc.tensor.matmul_mx(
+                    out=acc[:],
+                    lhsT=cw[:, j * P : (j + 1) * P].bitcast(FP8X4),
+                    lhsT_scale=sc[:, j * P : (j + 1) * P],
+                    rhs=wc[:].bitcast(FP8X4),
+                    rhs_scale=ws[:],
+                    start=True,
+                    stop=True,
+                )
+                res[j] = acc
+            return res
+
+        def a1(g, j):
+            if j == 0:
+                X1[g] = x1pool.tile([P, 2, D], F32, name="x1", tag="x1")
+            i = 2 * g + j
+            nc.vector.scalar_tensor_tensor(
+                out=X1[g][:, j, :], in0=Y[g][j][:], scalar=c32[:, 2 * i : 2 * i + 1],
+                in1=x_bf(i), op0=MULT, op1=ADD,
+            )
+
+        def t1(g):
+            res = []
+            for j in range(2):
+                t = ps_t.tile([P, 4, P], F32, name="t1", tag="t1")
+                for q in range(4):
+                    nc.tensor.transpose(t[:, q, :], X1[g][:, j, q::4], ident[:])
+                res.append(t)
+            T1[g] = res
+
+        def e1(g):
+            g1 = gpool.tile([P, 8 * P], BF16, name="g1", tag="g1", align_bytes=64)
+            for j in range(2):
+                nc.scalar.copy(
+                    out=g1[:, j * D : (j + 1) * D].rearrange("p (k t) -> p k t", t=4),
+                    in_=T1[g][j][:].rearrange("p t k -> p k t"),
+                )
+            G1[g] = g1
+
+        def a2v(g, j):
+            if j == 0:
+                O[g] = opool.tile([P, 2, D], F32, name="o", tag="o")
+            i = 2 * g + j
+            nc.vector.scalar_tensor_tensor(
+                out=O[g][:, j, :], in0=Z[g][j][:], scalar=c32[:, 2 * i + 1 : 2 * i + 2],
+                in1=X1[g][:, j, :], op0=MULT, op1=ADD,
+            )
+
+        def cz(g):
+            i = 2 * g + 1
+            t = czpool.tile([P, D], F32, name="cz", tag="cz")
+            nc.scalar.activation(
+                out=t[:], in_=Z[g][1][:], func=COPY, scale=c32[:, 2 * i + 1 : 2 * i + 2]
+            )
+            CZ[g] = t
+
+        def ga(g):
+            nc.gpsimd.tensor_tensor(out=O[g][:, 1, :], in0=CZ[g][:], in1=X1[g][:, 1, :], op=ADD)
+
+        def store(g, lo, hi):
+            nc.sync.dma_start(
+                out=o_dram[:, (2 * g + lo) * D : (2 * g + hi) * D],
+                in_=O[g][:, lo:hi, :].rearrange("p j d -> p (j d)"),
+            )
+
+        def off(g):
+            return g < NP - 1
+
+        def ok(g):
+            return 0 <= g < NP
+
+        for it in range(-2, NP + 3):
+            if ok(it - 2):
+                t1(it - 2)
+                e1(it - 2)
+            if ok(it):
+                Y[it] = mm(ps_y, "y", QX[it], w0c, w0s)
+            if ok(it - 3):
+                Z[it - 3] = mm(ps_z, "z", Q1[it - 3], w1c, w1s)
+            if ok(it + 2):
+                tx(it + 2)
+            if ok(it - 3) and off(it - 3):
+                cz(it - 3)
+            if ok(it + 2):
+                ex(it + 2)
+            if it == -1 or it == 0:
+                h = (it + 1) * (D // 2)
+                nc.scalar.copy(
+                    out=w1g[:, h : h + D // 2, :].rearrange("p (c i) t -> p c t i", i=4),
+                    in_=w1r[:, :, h : h + D // 2].rearrange("p t (c i) -> p c t i", i=4),
+                )
+            if ok(it):
+                a1(it, 0)
+            if ok(it + 1):
+                QX[it + 1] = quant(GX[it + 1], "cx", "sx")
+            if ok(it - 2):
+                Q1[it - 2] = quant(G1[it - 2], "c1", "s1")
+            if ok(it):
+                a1(it, 1)
+            if it == 1:
+                nc.vector.quantize_mx(
+                    out=w1c[:].bitcast(FP8X4), scales=w1s[:],
+                    in_=w1g[:].rearrange("p n t -> p (n t)"),
+                )
+            if ok(it - 3):
+                a2v(it - 3, 0)
+                if off(it - 3):
+                    ga(it - 3)
+                    store(it - 3, 0, 2)
+                else:
+                    store(it - 3, 0, 1)
+                    a2v(it - 3, 1)
+                    store(it - 3, 1, 2)

@@ -33,6 +33,7 @@ def tile_precomputedmetanet_pa_t_kernel(tc, transformed, coeff, task_mats, out):
         const = ctx.enter_context(tc.tile_pool(name="const", bufs=1))
         gpool = ctx.enter_context(tc.tile_pool(name="gpool", bufs=3))
         qpool = ctx.enter_context(tc.tile_pool(name="qpool", bufs=3))
+        bpool = ctx.enter_context(tc.tile_pool(name="bpool", bufs=3))
         x1pool = ctx.enter_context(tc.tile_pool(name="x1pool", bufs=6))
         opool = ctx.enter_context(tc.tile_pool(name="opool", bufs=6))
         czpool = ctx.enter_context(tc.tile_pool(name="czpool", bufs=3))
@@ -100,6 +101,7 @@ def tile_precomputedmetanet_pa_t_kernel(tc, transformed, coeff, task_mats, out):
         QX = {}
         Y = {}
         X1 = {}
+        X1B = {}
         T1 = {}
         G1 = {}
         Q1 = {}
@@ -154,22 +156,38 @@ def tile_precomputedmetanet_pa_t_kernel(tc, transformed, coeff, task_mats, out):
                 in1=x_bf(i), op0=MULT, op1=ADD,
             )
 
+        def cast_views(g, j):
+            if g not in X1B:
+                X1B[g] = bpool.tile([P, 2 * D], BF16, name="x1b", tag="x1b")
+            dst = X1B[g][:, j * D : (j + 1) * D].rearrange("p (u m e) -> p u m e", u=2, e=2)
+            src = X1[g][:, j, :].rearrange("p (m u e) -> p u m e", u=2, e=2)
+            return dst, src
+
+        def cast_s(g, j):
+            dst, src = cast_views(g, j)
+            nc.scalar.copy(out=dst, in_=src)
+
+        def cast_g(g, j):
+            dst, src = cast_views(g, j)
+            nc.gpsimd.tensor_scalar(
+                out=dst, in0=src, scalar1=1.0, scalar2=0.0, op0=MULT, op1=ADD
+            )
+
         def t1(g):
-            res = []
+            t = ps_t.tile([P, 2, 2, P], F32, name="t1", tag="t1")
+            words = X1B[g][:].bitcast(F32)
             for j in range(2):
-                t = ps_t.tile([P, 4, P], F32, name="t1", tag="t1")
-                for q in range(4):
-                    nc.tensor.transpose(t[:, q, :], X1[g][:, j, q::4], ident[:])
-                res.append(t)
-            T1[g] = res
+                for u in range(2):
+                    lo = (2 * j + u) * P
+                    nc.tensor.transpose(t[:, j, u, :], words[:, lo : lo + P], ident[:])
+            T1[g] = t
 
         def e1(g):
             g1 = gpool.tile([P, 8 * P], BF16, name="g1", tag="g1", align_bytes=64)
-            for j in range(2):
-                nc.scalar.copy(
-                    out=g1[:, j * D : (j + 1) * D].rearrange("p (k t) -> p k t", t=4),
-                    in_=T1[g][j][:].rearrange("p t k -> p k t"),
-                )
+            nc.scalar.copy(
+                out=g1[:].bitcast(F32).rearrange("p (j k u) -> p j k u", j=2, u=2),
+                in_=T1[g][:].rearrange("p j u k -> p j k u"),
+            )
             G1[g] = g1
 
         def a2v(g, j):
@@ -208,6 +226,8 @@ def tile_precomputedmetanet_pa_t_kernel(tc, transformed, coeff, task_mats, out):
             if ok(it - 2):
                 t1(it - 2)
                 e1(it - 2)
+            if ok(it - 1):
+                cast_s(it - 1, 0)
             if ok(it):
                 Y[it] = mm(ps_y, "y", QX[it], w0c, w0s)
             if ok(it - 3):
@@ -226,12 +246,11 @@ def tile_precomputedmetanet_pa_t_kernel(tc, transformed, coeff, task_mats, out):
                 )
             if ok(it):
                 a1(it, 0)
+                a1(it, 1)
             if ok(it + 1):
                 QX[it + 1] = quant(GX[it + 1], "cx", "sx")
             if ok(it - 2):
                 Q1[it - 2] = quant(G1[it - 2], "c1", "s1")
-            if ok(it):
-                a1(it, 1)
             if it == 1:
                 nc.vector.quantize_mx(
                     out=w1c[:].bitcast(FP8X4), scales=w1s[:],
@@ -246,3 +265,5 @@ def tile_precomputedmetanet_pa_t_kernel(tc, transformed, coeff, task_mats, out):
                     store(it - 3, 0, 1)
                     a2v(it - 3, 1)
                     store(it - 3, 1, 2)
+            if ok(it):
+                cast_g(it, 1)

@@ -47,7 +47,6 @@ def tile_precomputedmetanet_pa_t_kernel(tc, transformed, coeff, task_mats, out):
         make_identity(nc, ident[:])
 
         w0r = const.tile([P, 4, D], BF16, name="w0r")
-        nc.sync.dma_start(out=w0r[:], in_=task_mats[0].rearrange("(p t) n -> p t n", t=4))
         xs = []
         where = {}
         start = 0
@@ -61,8 +60,10 @@ def tile_precomputedmetanet_pa_t_kernel(tc, transformed, coeff, task_mats, out):
                 where[start + k] = (c, k)
             start += n
             if c == 0:
-                nc.sync.dma_start(out=c_bf[:], in_=c_dram)
+                nc.sync.dma_start(out=w0r[:], in_=task_mats[0].rearrange("(p t) n -> p t n", t=4))
             if c == 1:
+                nc.sync.dma_start(out=c_bf[:], in_=c_dram)
+            if c == 2:
                 nc.sync.dma_start(out=w1r[:], in_=task_mats[1].rearrange("(p t) n -> p t n", t=4))
         assert start == NT
 
@@ -173,6 +174,13 @@ def tile_precomputedmetanet_pa_t_kernel(tc, transformed, coeff, task_mats, out):
                 out=dst, in0=src, scalar1=1.0, scalar2=0.0, op0=MULT, op1=ADD
             )
 
+        def cast_v(g, j):
+            dst, src = cast_views(g, j)
+            nc.vector.tensor_copy(out=dst, in_=src)
+
+        def caster(g):
+            return "vgs"[g % 3]
+
         def t1(g):
             t = ps_t.tile([P, 2, 2, P], F32, name="t1", tag="t1")
             words = X1B[g][:].bitcast(F32)
@@ -222,22 +230,25 @@ def tile_precomputedmetanet_pa_t_kernel(tc, transformed, coeff, task_mats, out):
         def ok(g):
             return 0 <= g < NP
 
-        for it in range(-2, NP + 3):
+        for it in range(-3, NP + 3):
             if ok(it - 2):
                 t1(it - 2)
+            if ok(it - 2):
                 e1(it - 2)
             if ok(it - 1):
                 cast_s(it - 1, 0)
+            if ok(it - 1) and caster(it - 1) == "s":
+                cast_s(it - 1, 1)
             if ok(it):
                 Y[it] = mm(ps_y, "y", QX[it], w0c, w0s)
             if ok(it - 3):
                 Z[it - 3] = mm(ps_z, "z", Q1[it - 3], w1c, w1s)
-            if ok(it + 2):
-                tx(it + 2)
+            if ok(it + 3):
+                tx(it + 3)
             if ok(it - 3) and off(it - 3):
                 cz(it - 3)
-            if ok(it + 2):
-                ex(it + 2)
+            if ok(it + 3):
+                ex(it + 3)
             if it == -1 or it == 0:
                 h = (it + 1) * (D // 2)
                 nc.scalar.copy(
@@ -246,9 +257,10 @@ def tile_precomputedmetanet_pa_t_kernel(tc, transformed, coeff, task_mats, out):
                 )
             if ok(it):
                 a1(it, 0)
+            if ok(it):
                 a1(it, 1)
-            if ok(it + 1):
-                QX[it + 1] = quant(GX[it + 1], "cx", "sx")
+            if ok(it + 2):
+                QX[it + 2] = quant(GX[it + 2], "cx", "sx")
             if ok(it - 2):
                 Q1[it - 2] = quant(G1[it - 2], "c1", "s1")
             if it == 1:
@@ -256,14 +268,16 @@ def tile_precomputedmetanet_pa_t_kernel(tc, transformed, coeff, task_mats, out):
                     out=w1c[:].bitcast(FP8X4), scales=w1s[:],
                     in_=w1g[:].rearrange("p n t -> p (n t)"),
                 )
+            if ok(it) and caster(it) == "v":
+                cast_v(it, 1)
             if ok(it - 3):
                 a2v(it - 3, 0)
-                if off(it - 3):
-                    ga(it - 3)
-                    store(it - 3, 0, 2)
-                else:
-                    store(it - 3, 0, 1)
-                    a2v(it - 3, 1)
-                    store(it - 3, 1, 2)
-            if ok(it):
+            if ok(it - 3) and off(it - 3):
+                ga(it - 3)
+                store(it - 3, 0, 2)
+            if ok(it - 3) and not off(it - 3):
+                store(it - 3, 0, 1)
+                a2v(it - 3, 1)
+                store(it - 3, 1, 2)
+            if ok(it) and caster(it) == "g":
                 cast_g(it, 1)

@@ -19,7 +19,7 @@ NT = B // P
 NP = NT // 2
 FLOPS = 2 * 2 * B * D * D
 
-CHUNKS = [2, 2, 4, 8, 8, 8, 8, 8, 8, 8]
+CHUNKS = [2, 2, 2, 2, 2, 2, 4, 4, 4, 8, 8, 8, 8, 8]
 W0_SPLIT = 384
 
 
@@ -63,7 +63,7 @@ def tile_precomputedmetanet_pa_t_kernel(tc, transformed, coeff, task_mats, out):
                 nc.sync.dma_start(out=w0r[:], in_=task_mats[0].rearrange("(p t) n -> p t n", t=4))
             if c == 1:
                 nc.sync.dma_start(out=c_bf[:], in_=c_dram)
-            if c == 2:
+            if c == 3:
                 nc.sync.dma_start(out=w1r[:], in_=task_mats[1].rearrange("(p t) n -> p t n", t=4))
         assert start == NT
 
@@ -83,19 +83,6 @@ def tile_precomputedmetanet_pa_t_kernel(tc, transformed, coeff, task_mats, out):
         w1c = const.tile([P, D], U32, name="w1c", align_bytes=64)
         w1s = const.tile([P, D], U8, name="w1s", align_bytes=64)
         c32 = const.tile([P, 2 * NT], F32, name="c32")
-
-        nc.vector.tensor_copy(
-            out=w0g[:, 0:W0_SPLIT, :].rearrange("p (c i) t -> p c t i", i=4),
-            in_=w0r[:, :, 0:W0_SPLIT].rearrange("p t (c i) -> p c t i", i=4),
-        )
-        nc.scalar.copy(
-            out=w0g[:, W0_SPLIT:D, :].rearrange("p (c i) t -> p c t i", i=4),
-            in_=w0r[:, :, W0_SPLIT:D].rearrange("p t (c i) -> p c t i", i=4),
-        )
-        nc.vector.tensor_copy(out=c32[:], in_=c_bf[:])
-        nc.vector.quantize_mx(
-            out=w0c[:].bitcast(FP8X4), scales=w0s[:], in_=w0g[:].rearrange("p n t -> p (n t)")
-        )
 
         TPX = {}
         GX = {}
@@ -168,18 +155,12 @@ def tile_precomputedmetanet_pa_t_kernel(tc, transformed, coeff, task_mats, out):
             dst, src = cast_views(g, j)
             nc.scalar.copy(out=dst, in_=src)
 
-        def cast_g(g, j):
-            dst, src = cast_views(g, j)
-            nc.gpsimd.tensor_scalar(
-                out=dst, in0=src, scalar1=1.0, scalar2=0.0, op0=MULT, op1=ADD
-            )
-
         def cast_v(g, j):
             dst, src = cast_views(g, j)
             nc.vector.tensor_copy(out=dst, in_=src)
 
         def caster(g):
-            return "vgs"[g % 3]
+            return "vs"[g % 2]
 
         def t1(g):
             t = ps_t.tile([P, 2, 2, P], F32, name="t1", tag="t1")
@@ -230,7 +211,22 @@ def tile_precomputedmetanet_pa_t_kernel(tc, transformed, coeff, task_mats, out):
         def ok(g):
             return 0 <= g < NP
 
-        for it in range(-3, NP + 3):
+        tx(0)
+        ex(0)
+        nc.vector.tensor_copy(
+            out=w0g[:, 0:W0_SPLIT, :].rearrange("p (c i) t -> p c t i", i=4),
+            in_=w0r[:, :, 0:W0_SPLIT].rearrange("p t (c i) -> p c t i", i=4),
+        )
+        nc.scalar.copy(
+            out=w0g[:, W0_SPLIT:D, :].rearrange("p (c i) t -> p c t i", i=4),
+            in_=w0r[:, :, W0_SPLIT:D].rearrange("p t (c i) -> p c t i", i=4),
+        )
+        nc.vector.tensor_copy(out=c32[:], in_=c_bf[:])
+        nc.vector.quantize_mx(
+            out=w0c[:].bitcast(FP8X4), scales=w0s[:], in_=w0g[:].rearrange("p n t -> p (n t)")
+        )
+
+        for it in range(-2, NP):
             if ok(it - 2):
                 t1(it - 2)
             if ok(it - 2):
@@ -268,7 +264,7 @@ def tile_precomputedmetanet_pa_t_kernel(tc, transformed, coeff, task_mats, out):
                     out=w1c[:].bitcast(FP8X4), scales=w1s[:],
                     in_=w1g[:].rearrange("p n t -> p (n t)"),
                 )
-            if ok(it) and caster(it) == "v":
+            if ok(it) and it < NP - 1 and caster(it) == "v":
                 cast_v(it, 1)
             if ok(it - 3):
                 a2v(it - 3, 0)
@@ -279,5 +275,28 @@ def tile_precomputedmetanet_pa_t_kernel(tc, transformed, coeff, task_mats, out):
                 store(it - 3, 0, 1)
                 a2v(it - 3, 1)
                 store(it - 3, 1, 2)
-            if ok(it) and caster(it) == "g":
-                cast_g(it, 1)
+
+        g = NP - 1
+        t1(g - 1)
+        e1(g - 1)
+        cast_s(g, 0)
+        cast_v(g, 1)
+        Z[g - 2] = mm(ps_z, "z", Q1[g - 2], w1c, w1s)
+        t1(g)
+        cz(g - 2)
+        e1(g)
+        Q1[g - 1] = quant(G1[g - 1], "c1", "s1")
+        a2v(g - 2, 0)
+        ga(g - 2)
+        store(g - 2, 0, 2)
+        Z[g - 1] = mm(ps_z, "z", Q1[g - 1], w1c, w1s)
+        cz(g - 1)
+        Q1[g] = quant(G1[g], "c1", "s1")
+        a2v(g - 1, 0)
+        ga(g - 1)
+        store(g - 1, 0, 2)
+        Z[g] = mm(ps_z, "z", Q1[g], w1c, w1s)
+        a2v(g, 0)
+        store(g, 0, 1)
+        a2v(g, 1)
+        store(g, 1, 2)

@@ -160,23 +160,39 @@ def tile_precomputedmetanet_pa_t_kernel(tc, transformed, coeff, task_mats, out):
             nc.vector.tensor_copy(out=dst, in_=src)
 
         def caster(g):
-            return "vs"[g % 2]
+            return "vnn"[g % 3]
 
         def t1(g):
             t = ps_t.tile([P, 2, 2, P], F32, name="t1", tag="t1")
             words = X1B[g][:].bitcast(F32)
-            for j in range(2):
+            plain = caster(g) == "n"
+            for j in range(1 if plain else 2):
                 for u in range(2):
                     lo = (2 * j + u) * P
                     nc.tensor.transpose(t[:, j, u, :], words[:, lo : lo + P], ident[:])
-            T1[g] = t
+            T1[g] = [t]
+            if plain:
+                t2 = ps_t.tile([P, 4, P], F32, name="t1", tag="t1")
+                for q in range(4):
+                    nc.tensor.transpose(t2[:, q, :], X1[g][:, 1, q::4], ident[:])
+                T1[g].append(t2)
 
         def e1(g):
             g1 = gpool.tile([P, 8 * P], BF16, name="g1", tag="g1", align_bytes=64)
-            nc.scalar.copy(
-                out=g1[:].bitcast(F32).rearrange("p (j k u) -> p j k u", j=2, u=2),
-                in_=T1[g][:].rearrange("p j u k -> p j k u"),
-            )
+            if len(T1[g]) == 1:
+                nc.scalar.copy(
+                    out=g1[:].bitcast(F32).rearrange("p (j k u) -> p j k u", j=2, u=2),
+                    in_=T1[g][0][:].rearrange("p j u k -> p j k u"),
+                )
+            else:
+                nc.scalar.copy(
+                    out=g1[:, 0:D].bitcast(F32).rearrange("p (k u) -> p k u", u=2),
+                    in_=T1[g][0][:, 0].rearrange("p u k -> p k u"),
+                )
+                nc.scalar.copy(
+                    out=g1[:, D : 2 * D].rearrange("p (k t) -> p k t", t=4),
+                    in_=T1[g][1][:].rearrange("p t k -> p k t"),
+                )
             G1[g] = g1
 
         def a2v(g, j):
@@ -226,21 +242,19 @@ def tile_precomputedmetanet_pa_t_kernel(tc, transformed, coeff, task_mats, out):
             out=w0c[:].bitcast(FP8X4), scales=w0s[:], in_=w0g[:].rearrange("p n t -> p (n t)")
         )
 
-        for it in range(-2, NP):
+        for it in range(-2, NP + 3):
             if ok(it - 2):
                 t1(it - 2)
-            if ok(it - 2):
-                e1(it - 2)
-            if ok(it - 1):
-                cast_s(it - 1, 0)
-            if ok(it - 1) and caster(it - 1) == "s":
-                cast_s(it - 1, 1)
             if ok(it):
                 Y[it] = mm(ps_y, "y", QX[it], w0c, w0s)
             if ok(it - 3):
                 Z[it - 3] = mm(ps_z, "z", Q1[it - 3], w1c, w1s)
             if ok(it + 3):
                 tx(it + 3)
+            if ok(it - 1):
+                cast_s(it - 1, 0)
+            if ok(it - 2):
+                e1(it - 2)
             if ok(it - 3) and off(it - 3):
                 cz(it - 3)
             if ok(it + 3):
@@ -264,39 +278,14 @@ def tile_precomputedmetanet_pa_t_kernel(tc, transformed, coeff, task_mats, out):
                     out=w1c[:].bitcast(FP8X4), scales=w1s[:],
                     in_=w1g[:].rearrange("p n t -> p (n t)"),
                 )
-            if ok(it) and it < NP - 1 and caster(it) == "v":
+            if ok(it) and caster(it) == "v":
                 cast_v(it, 1)
             if ok(it - 3):
                 a2v(it - 3, 0)
             if ok(it - 3) and off(it - 3):
                 ga(it - 3)
+            if ok(it - 3) and off(it - 3):
                 store(it - 3, 0, 2)
             if ok(it - 3) and not off(it - 3):
-                store(it - 3, 0, 1)
                 a2v(it - 3, 1)
-                store(it - 3, 1, 2)
-
-        g = NP - 1
-        t1(g - 1)
-        e1(g - 1)
-        cast_s(g, 0)
-        cast_v(g, 1)
-        Z[g - 2] = mm(ps_z, "z", Q1[g - 2], w1c, w1s)
-        t1(g)
-        cz(g - 2)
-        e1(g)
-        Q1[g - 1] = quant(G1[g - 1], "c1", "s1")
-        a2v(g - 2, 0)
-        ga(g - 2)
-        store(g - 2, 0, 2)
-        Z[g - 1] = mm(ps_z, "z", Q1[g - 1], w1c, w1s)
-        cz(g - 1)
-        Q1[g] = quant(G1[g], "c1", "s1")
-        a2v(g - 1, 0)
-        ga(g - 1)
-        store(g - 1, 0, 2)
-        Z[g] = mm(ps_z, "z", Q1[g], w1c, w1s)
-        a2v(g, 0)
-        store(g, 0, 1)
-        a2v(g, 1)
-        store(g, 1, 2)
+                store(it - 3, 0, 2)

@@ -21,6 +21,7 @@ FLOPS = 2 * 2 * B * D * D
 
 CHUNKS = [2, 2, 2, 2, 2, 2, 4, 4, 4, 8, 8, 8, 8, 8]
 W0_SPLIT = 384
+X1_BUFS = 28
 
 
 def tile_precomputedmetanet_pa_t_kernel(tc, transformed, coeff, task_mats, out):
@@ -34,9 +35,7 @@ def tile_precomputedmetanet_pa_t_kernel(tc, transformed, coeff, task_mats, out):
         gpool = ctx.enter_context(tc.tile_pool(name="gpool", bufs=3))
         qpool = ctx.enter_context(tc.tile_pool(name="qpool", bufs=3))
         bpool = ctx.enter_context(tc.tile_pool(name="bpool", bufs=3))
-        x1pool = ctx.enter_context(tc.tile_pool(name="x1pool", bufs=6))
-        opool = ctx.enter_context(tc.tile_pool(name="opool", bufs=6))
-        czpool = ctx.enter_context(tc.tile_pool(name="czpool", bufs=3))
+        x1pool = ctx.enter_context(tc.tile_pool(name="x1pool", bufs=X1_BUFS))
         ps_x = ctx.enter_context(tc.psum_pool(name="ps_x", bufs=2))
         ps_t = ctx.enter_context(tc.psum_pool(name="ps_t", bufs=2))
         ps_y = ctx.enter_context(tc.psum_pool(name="ps_y", bufs=2))
@@ -94,7 +93,6 @@ def tile_precomputedmetanet_pa_t_kernel(tc, transformed, coeff, task_mats, out):
         G1 = {}
         Q1 = {}
         Z = {}
-        O = {}
         CZ = {}
 
         def tx(g):
@@ -160,7 +158,7 @@ def tile_precomputedmetanet_pa_t_kernel(tc, transformed, coeff, task_mats, out):
             nc.vector.tensor_copy(out=dst, in_=src)
 
         def caster(g):
-            return "vnn"[g % 3]
+            return "vn"[g % 2]
 
         def t1(g):
             t = ps_t.tile([P, 2, 2, P], F32, name="t1", tag="t1")
@@ -195,34 +193,82 @@ def tile_precomputedmetanet_pa_t_kernel(tc, transformed, coeff, task_mats, out):
                 )
             G1[g] = g1
 
-        def a2v(g, j):
+        def t1_tile(g, j):
             if j == 0:
-                O[g] = opool.tile([P, 2, D], F32, name="o", tag="o")
+                t = ps_t.tile([P, 2, P], F32, name="t1", tag="t1")
+                words = X1B[g][:].bitcast(F32)
+                for u in range(2):
+                    nc.tensor.transpose(t[:, u, :], words[:, u * P : (u + 1) * P], ident[:])
+            else:
+                t = ps_t.tile([P, 4, P], F32, name="t1", tag="t1")
+                for q in range(4):
+                    nc.tensor.transpose(t[:, q, :], X1[g][:, 1, q::4], ident[:])
+            T1[g, j] = t
+
+        def e1_tile(g, j):
+            if j == 0:
+                G1[g] = gpool.tile([P, 8 * P], BF16, name="g1", tag="g1", align_bytes=64)
+                nc.scalar.copy(
+                    out=G1[g][:, 0:D].bitcast(F32).rearrange("p (k u) -> p k u", u=2),
+                    in_=T1[g, 0][:].rearrange("p u k -> p k u"),
+                )
+            else:
+                nc.scalar.copy(
+                    out=G1[g][:, D : 2 * D].rearrange("p (k t) -> p k t", t=4),
+                    in_=T1[g, 1][:].rearrange("p t k -> p k t"),
+                )
+
+        def q1_tile(g, j):
+            if j == 0:
+                cw = qpool.tile([P, 2 * P], U32, name="c1", tag="c1", align_bytes=64)
+                sc = qpool.tile([P, 2 * P], U8, name="s1", tag="s1", align_bytes=64)
+                Q1[g] = (cw, sc)
+                Z[g] = {}
+            cw, sc = Q1[g]
+            nc.vector.quantize_mx(
+                out=cw[:, j * P : (j + 1) * P].bitcast(FP8X4),
+                scales=sc[:, j * P : (j + 1) * P],
+                in_=G1[g][:, j * D : (j + 1) * D],
+            )
+
+        def z_tile(g, j):
+            cw, sc = Q1[g]
+            acc = ps_y.tile([P, D], F32, name="y", tag="y")
+            nc.tensor.matmul_mx(
+                out=acc[:],
+                lhsT=cw[:, j * P : (j + 1) * P].bitcast(FP8X4),
+                lhsT_scale=sc[:, j * P : (j + 1) * P],
+                rhs=w1c[:].bitcast(FP8X4),
+                rhs_scale=w1s[:],
+                start=True,
+                stop=True,
+            )
+            Z[g][j] = acc
+
+        def a2v(g, j):
             i = 2 * g + j
             nc.vector.scalar_tensor_tensor(
-                out=O[g][:, j, :], in0=Z[g][j][:], scalar=c32[:, 2 * i + 1 : 2 * i + 2],
+                out=X1[g][:, j, :], in0=Z[g][j][:], scalar=c32[:, 2 * i + 1 : 2 * i + 2],
                 in1=X1[g][:, j, :], op0=MULT, op1=ADD,
             )
 
         def cz(g):
             i = 2 * g + 1
-            t = czpool.tile([P, D], F32, name="cz", tag="cz")
+            c, k = where[2 * g]
+            t = xs[c][:, k * D : (k + 2) * D].bitcast(F32)
             nc.scalar.activation(
-                out=t[:], in_=Z[g][1][:], func=COPY, scale=c32[:, 2 * i + 1 : 2 * i + 2]
+                out=t, in_=Z[g][1][:], func=COPY, scale=c32[:, 2 * i + 1 : 2 * i + 2]
             )
             CZ[g] = t
 
         def ga(g):
-            nc.gpsimd.tensor_tensor(out=O[g][:, 1, :], in0=CZ[g][:], in1=X1[g][:, 1, :], op=ADD)
+            nc.gpsimd.tensor_tensor(out=X1[g][:, 1, :], in0=CZ[g], in1=X1[g][:, 1, :], op=ADD)
 
         def store(g, lo, hi):
             nc.sync.dma_start(
                 out=o_dram[:, (2 * g + lo) * D : (2 * g + hi) * D],
-                in_=O[g][:, lo:hi, :].rearrange("p j d -> p (j d)"),
+                in_=X1[g][:, lo:hi, :].rearrange("p j d -> p (j d)"),
             )
-
-        def off(g):
-            return g < NP - 1
 
         def ok(g):
             return 0 <= g < NP
@@ -242,7 +288,7 @@ def tile_precomputedmetanet_pa_t_kernel(tc, transformed, coeff, task_mats, out):
             out=w0c[:].bitcast(FP8X4), scales=w0s[:], in_=w0g[:].rearrange("p n t -> p (n t)")
         )
 
-        for it in range(-2, NP + 3):
+        for it in range(-2, NP):
             if ok(it - 2):
                 t1(it - 2)
             if ok(it):
@@ -255,7 +301,7 @@ def tile_precomputedmetanet_pa_t_kernel(tc, transformed, coeff, task_mats, out):
                 cast_s(it - 1, 0)
             if ok(it - 2):
                 e1(it - 2)
-            if ok(it - 3) and off(it - 3):
+            if ok(it - 3):
                 cz(it - 3)
             if ok(it + 3):
                 ex(it + 3)
@@ -282,10 +328,32 @@ def tile_precomputedmetanet_pa_t_kernel(tc, transformed, coeff, task_mats, out):
                 cast_v(it, 1)
             if ok(it - 3):
                 a2v(it - 3, 0)
-            if ok(it - 3) and off(it - 3):
+            if ok(it - 3):
                 ga(it - 3)
-            if ok(it - 3) and off(it - 3):
                 store(it - 3, 0, 2)
-            if ok(it - 3) and not off(it - 3):
-                a2v(it - 3, 1)
-                store(it - 3, 0, 2)
+
+        g = NP - 1
+        cast_s(g, 0)
+        t1(g - 1)
+        e1(g - 1)
+        Z[g - 2] = mm(ps_z, "z", Q1[g - 2], w1c, w1s)
+        t1_tile(g, 0)
+        t1_tile(g, 1)
+        e1_tile(g, 0)
+        e1_tile(g, 1)
+        a2v(g - 2, 1)
+        a2v(g - 2, 0)
+        store(g - 2, 0, 2)
+        Q1[g - 1] = quant(G1[g - 1], "c1", "s1")
+        Z[g - 1] = mm(ps_z, "z", Q1[g - 1], w1c, w1s)
+        q1_tile(g, 0)
+        q1_tile(g, 1)
+        z_tile(g, 0)
+        z_tile(g, 1)
+        a2v(g - 1, 1)
+        a2v(g - 1, 0)
+        store(g - 1, 0, 2)
+        a2v(g, 0)
+        store(g, 0, 1)
+        a2v(g, 1)
+        store(g, 1, 2)

@@ -21,7 +21,8 @@ FLOPS = 2 * 2 * B * D * D
 
 CHUNKS = [2, 2, 2, 2, 2, 2, 4, 4, 4, 8, 8, 8, 8, 8]
 W0_SPLIT = 384
-X1_BUFS = 28
+X1_BUFS = 20
+RULE = "vvnvn"
 
 
 def tile_precomputedmetanet_pa_t_kernel(tc, transformed, coeff, task_mats, out):
@@ -32,8 +33,8 @@ def tile_precomputedmetanet_pa_t_kernel(tc, transformed, coeff, task_mats, out):
 
     with ExitStack() as ctx:
         const = ctx.enter_context(tc.tile_pool(name="const", bufs=1))
-        gpool = ctx.enter_context(tc.tile_pool(name="gpool", bufs=3))
-        qpool = ctx.enter_context(tc.tile_pool(name="qpool", bufs=3))
+        gpool = ctx.enter_context(tc.tile_pool(name="gpool", bufs=8))
+        qpool = ctx.enter_context(tc.tile_pool(name="qpool", bufs=4))
         bpool = ctx.enter_context(tc.tile_pool(name="bpool", bufs=3))
         x1pool = ctx.enter_context(tc.tile_pool(name="x1pool", bufs=X1_BUFS))
         ps_x = ctx.enter_context(tc.psum_pool(name="ps_x", bufs=2))
@@ -83,14 +84,16 @@ def tile_precomputedmetanet_pa_t_kernel(tc, transformed, coeff, task_mats, out):
         w1s = const.tile([P, D], U8, name="w1s", align_bytes=64)
         c32 = const.tile([P, 2 * NT], F32, name="c32")
 
+        def ok(g):
+            return 0 <= g < NP
+
         TPX = {}
-        GX = {}
+        GR = {}
         QX = {}
         Y = {}
         X1 = {}
         X1B = {}
         T1 = {}
-        G1 = {}
         Q1 = {}
         Z = {}
         CZ = {}
@@ -103,18 +106,28 @@ def tile_precomputedmetanet_pa_t_kernel(tc, transformed, coeff, task_mats, out):
             TPX[g] = t
 
         def ex(g):
-            gx = gpool.tile([P, 8 * P], BF16, name="gx", tag="gx", align_bytes=64)
             nc.scalar.copy(
-                out=gx[:].bitcast(F32).rearrange("p (j k u) -> p j k u", j=2, u=2),
+                out=grouped(g - 2, 0).bitcast(F32).rearrange("p (j k u) -> p j k u", j=2, u=2),
                 in_=TPX[g][:].rearrange("p j u k -> p j k u"),
             )
-            GX[g] = gx
 
-        def quant(src, tagc, tags):
-            cw = qpool.tile([P, 2 * P], U32, name=tagc, tag=tagc, align_bytes=64)
-            sc = qpool.tile([P, 2 * P], U8, name=tags, tag=tags, align_bytes=64)
-            nc.vector.quantize_mx(out=cw[:].bitcast(FP8X4), scales=sc[:], in_=src[:])
-            return (cw, sc)
+        def grouped(step, half):
+            if step not in GR:
+                GR[step] = gpool.tile([P, 16 * P], BF16, name="gr", tag="gr", align_bytes=64)
+            return GR[step][:, half * 8 * P : (half + 1) * 8 * P]
+
+        def quant(step):
+            lo = 0 if ok(step + 2) else 2 * P
+            hi = 4 * P if ok(step - 2) else 2 * P
+            cw = qpool.tile([P, 4 * P], U32, name="cw", tag="cw", align_bytes=64)
+            sc = qpool.tile([P, 4 * P], U8, name="sc", tag="sc", align_bytes=64)
+            for at in range(lo, hi, 2 * P):
+                nc.vector.quantize_mx(
+                    out=cw[:, at : at + 2 * P].bitcast(FP8X4), scales=sc[:, at : at + 2 * P],
+                    in_=GR[step][:, 4 * at : 4 * at + 8 * P],
+                )
+            QX[step + 2] = (cw[:, 0 : 2 * P], sc[:, 0 : 2 * P])
+            Q1[step - 2] = (cw[:, 2 * P : 4 * P], sc[:, 2 * P : 4 * P])
 
         def mm(pool, tag, q, wc, ws):
             res = {}
@@ -158,7 +171,7 @@ def tile_precomputedmetanet_pa_t_kernel(tc, transformed, coeff, task_mats, out):
             nc.vector.tensor_copy(out=dst, in_=src)
 
         def caster(g):
-            return "vn"[g % 2]
+            return "n" if g == NP - 1 else RULE[g % len(RULE)]
 
         def t1(g):
             t = ps_t.tile([P, 2, 2, P], F32, name="t1", tag="t1")
@@ -176,10 +189,10 @@ def tile_precomputedmetanet_pa_t_kernel(tc, transformed, coeff, task_mats, out):
                 T1[g].append(t2)
 
         def e1(g):
-            g1 = gpool.tile([P, 8 * P], BF16, name="g1", tag="g1", align_bytes=64)
+            g1 = grouped(g + 2, 1)
             if len(T1[g]) == 1:
                 nc.scalar.copy(
-                    out=g1[:].bitcast(F32).rearrange("p (j k u) -> p j k u", j=2, u=2),
+                    out=g1.bitcast(F32).rearrange("p (j k u) -> p j k u", j=2, u=2),
                     in_=T1[g][0][:].rearrange("p j u k -> p j k u"),
                 )
             else:
@@ -191,7 +204,6 @@ def tile_precomputedmetanet_pa_t_kernel(tc, transformed, coeff, task_mats, out):
                     out=g1[:, D : 2 * D].rearrange("p (k t) -> p k t", t=4),
                     in_=T1[g][1][:].rearrange("p t k -> p k t"),
                 )
-            G1[g] = g1
 
         def t1_tile(g, j):
             if j == 0:
@@ -207,14 +219,13 @@ def tile_precomputedmetanet_pa_t_kernel(tc, transformed, coeff, task_mats, out):
 
         def e1_tile(g, j):
             if j == 0:
-                G1[g] = gpool.tile([P, 8 * P], BF16, name="g1", tag="g1", align_bytes=64)
                 nc.scalar.copy(
-                    out=G1[g][:, 0:D].bitcast(F32).rearrange("p (k u) -> p k u", u=2),
+                    out=grouped(g + 2, 1)[:, 0:D].bitcast(F32).rearrange("p (k u) -> p k u", u=2),
                     in_=T1[g, 0][:].rearrange("p u k -> p k u"),
                 )
             else:
                 nc.scalar.copy(
-                    out=G1[g][:, D : 2 * D].rearrange("p (k t) -> p k t", t=4),
+                    out=grouped(g + 2, 1)[:, D : 2 * D].rearrange("p (k t) -> p k t", t=4),
                     in_=T1[g, 1][:].rearrange("p t k -> p k t"),
                 )
 
@@ -228,7 +239,7 @@ def tile_precomputedmetanet_pa_t_kernel(tc, transformed, coeff, task_mats, out):
             nc.vector.quantize_mx(
                 out=cw[:, j * P : (j + 1) * P].bitcast(FP8X4),
                 scales=sc[:, j * P : (j + 1) * P],
-                in_=G1[g][:, j * D : (j + 1) * D],
+                in_=grouped(g + 2, 1)[:, j * D : (j + 1) * D],
             )
 
         def z_tile(g, j):
@@ -261,17 +272,20 @@ def tile_precomputedmetanet_pa_t_kernel(tc, transformed, coeff, task_mats, out):
             )
             CZ[g] = t
 
-        def ga(g):
-            nc.gpsimd.tensor_tensor(out=X1[g][:, 1, :], in0=CZ[g], in1=X1[g][:, 1, :], op=ADD)
+        def ga(g, h):
+            o = grouped(h + 2, 1).bitcast(F32)
+            nc.gpsimd.tensor_tensor(out=o, in0=CZ[g], in1=X1[g][:, 1, :], op=ADD)
+            return o
+
+        def store_tile(g, j, src):
+            i = 2 * g + j
+            nc.sync.dma_start(out=o_dram[:, i * D : (i + 1) * D], in_=src)
 
         def store(g, lo, hi):
             nc.sync.dma_start(
                 out=o_dram[:, (2 * g + lo) * D : (2 * g + hi) * D],
                 in_=X1[g][:, lo:hi, :].rearrange("p j d -> p (j d)"),
             )
-
-        def ok(g):
-            return 0 <= g < NP
 
         tx(0)
         ex(0)
@@ -289,22 +303,24 @@ def tile_precomputedmetanet_pa_t_kernel(tc, transformed, coeff, task_mats, out):
         )
 
         for it in range(-2, NP):
+            if ok(it + 3) and it > 0:
+                tx(it + 3)
             if ok(it - 2):
                 t1(it - 2)
             if ok(it):
                 Y[it] = mm(ps_y, "y", QX[it], w0c, w0s)
             if ok(it - 3):
                 Z[it - 3] = mm(ps_z, "z", Q1[it - 3], w1c, w1s)
-            if ok(it + 3):
+            if it <= 0:
                 tx(it + 3)
             if ok(it - 1):
                 cast_s(it - 1, 0)
             if ok(it - 2):
                 e1(it - 2)
-            if ok(it - 3):
-                cz(it - 3)
             if ok(it + 3):
                 ex(it + 3)
+            if ok(it - 3):
+                cz(it - 3)
             if it == -1 or it == 0:
                 h = (it + 1) * (D // 2)
                 nc.scalar.copy(
@@ -315,10 +331,7 @@ def tile_precomputedmetanet_pa_t_kernel(tc, transformed, coeff, task_mats, out):
                 a1(it, 0)
             if ok(it):
                 a1(it, 1)
-            if ok(it + 2):
-                QX[it + 2] = quant(GX[it + 2], "cx", "sx")
-            if ok(it - 2):
-                Q1[it - 2] = quant(G1[it - 2], "c1", "s1")
+            quant(it)
             if it == 1:
                 nc.vector.quantize_mx(
                     out=w1c[:].bitcast(FP8X4), scales=w1s[:],
@@ -329,8 +342,8 @@ def tile_precomputedmetanet_pa_t_kernel(tc, transformed, coeff, task_mats, out):
             if ok(it - 3):
                 a2v(it - 3, 0)
             if ok(it - 3):
-                ga(it - 3)
-                store(it - 3, 0, 2)
+                store(it - 3, 0, 1)
+                store_tile(it - 3, 1, ga(it - 3, it - 2))
 
         g = NP - 1
         cast_s(g, 0)
@@ -341,10 +354,10 @@ def tile_precomputedmetanet_pa_t_kernel(tc, transformed, coeff, task_mats, out):
         t1_tile(g, 1)
         e1_tile(g, 0)
         e1_tile(g, 1)
+        quant(g + 1)
         a2v(g - 2, 1)
         a2v(g - 2, 0)
         store(g - 2, 0, 2)
-        Q1[g - 1] = quant(G1[g - 1], "c1", "s1")
         Z[g - 1] = mm(ps_z, "z", Q1[g - 1], w1c, w1s)
         q1_tile(g, 0)
         q1_tile(g, 1)

from contextlib import ExitStack

import concourse.mybir as mybir
from concourse.masks import make_identity

F32 = mybir.dt.float32
BF16 = mybir.dt.bfloat16
U32 = mybir.dt.uint32
U8 = mybir.dt.uint8
FP8X4 = mybir.dt.float8_e4m3fn_x4
MULT = mybir.AluOpType.mult
ADD = mybir.AluOpType.add
COPY = mybir.ActivationFunctionType.Copy

P = 128
B = 8192
D = 512
NT = B // P
NP = NT // 2
FLOPS = 2 * 2 * B * D * D

CHUNKS = [2, 2, 2, 2, 2, 2, 4, 4, 4, 8, 8, 8, 8, 8]
W0_SPLIT = 384
X1_BUFS = 20
RULE = "vvnvn"


def tile_precomputedmetanet_pa_t_kernel(tc, transformed, coeff, task_mats, out):
    nc = tc.nc
    x_dram = transformed.rearrange("(p i) d -> p (i d)", i=NT)
    o_dram = out.rearrange("(p i) d -> p (i d)", i=NT)
    c_dram = coeff.rearrange("(p i) c -> p (i c)", i=NT)

    with ExitStack() as ctx:
        const = ctx.enter_context(tc.tile_pool(name="const", bufs=1))
        gpool = ctx.enter_context(tc.tile_pool(name="gpool", bufs=8))
        qpool = ctx.enter_context(tc.tile_pool(name="qpool", bufs=4))
        bpool = ctx.enter_context(tc.tile_pool(name="bpool", bufs=3))
        x1pool = ctx.enter_context(tc.tile_pool(name="x1pool", bufs=X1_BUFS))
        ps_x = ctx.enter_context(tc.psum_pool(name="ps_x", bufs=2))
        ps_t = ctx.enter_context(tc.psum_pool(name="ps_t", bufs=2))
        ps_y = ctx.enter_context(tc.psum_pool(name="ps_y", bufs=2))
        ps_z = ctx.enter_context(tc.psum_pool(name="ps_z", bufs=2))
        ctx.enter_context(tc.manual_schedule())

        ident = const.tile([P, P], F32, name="ident")
        make_identity(nc, ident[:])

        w0r = const.tile([P, 4, D], BF16, name="w0r")
        xs = []
        where = {}
        start = 0
        w1r = const.tile([P, 4, D], BF16, name="w1r")
        c_bf = const.tile([P, 2 * NT], BF16, name="c_bf")
        for c, n in enumerate(CHUNKS):
            xc = const.tile([P, n * D], BF16, name="x%d" % c)
            nc.sync.dma_start(out=xc[:], in_=x_dram[:, start * D : (start + n) * D])
            xs.append(xc)
            for k in range(n):
                where[start + k] = (c, k)
            start += n
            if c == 0:
                nc.sync.dma_start(out=w0r[:], in_=task_mats[0].rearrange("(p t) n -> p t n", t=4))
            if c == 1:
                nc.sync.dma_start(out=c_bf[:], in_=c_dram)
            if c == 3:
                nc.sync.dma_start(out=w1r[:], in_=task_mats[1].rearrange("(p t) n -> p t n", t=4))
        assert start == NT

        def x_bf(i):
            c, k = where[i]
            return xs[c][:, k * D : (k + 1) * D]

        def x_words(i, u):
            c, k = where[i]
            lo = k * (D // 2)
            return xs[c][:].bitcast(F32)[:, lo + u : lo + 2 * P : 2]

        w0g = const.tile([P, D, 4], BF16, name="w0g", align_bytes=64)
        w0c = const.tile([P, D], U32, name="w0c", align_bytes=64)
        w0s = const.tile([P, D], U8, name="w0s", align_bytes=64)
        w1g = const.tile([P, D, 4], BF16, name="w1g", align_bytes=64)
        w1c = const.tile([P, D], U32, name="w1c", align_bytes=64)
        w1s = const.tile([P, D], U8, name="w1s", align_bytes=64)
        c32 = const.tile([P, 2 * NT], F32, name="c32")

        def ok(g):
            return 0 <= g < NP

        TPX = {}
        GR = {}
        QX = {}
        Y = {}
        X1 = {}
        X1B = {}
        T1 = {}
        Q1 = {}
        Z = {}
        CZ = {}

        def tx(g):
            t = ps_x.tile([P, 2, 2, P], F32, name="tpx", tag="tpx")
            for j in range(2):
                for u in range(2):
                    nc.tensor.transpose(t[:, j, u, :], x_words(2 * g + j, u), ident[:])
            TPX[g] = t

        def ex(g):
            nc.scalar.copy(
                out=grouped(g - 2, 0).bitcast(F32).rearrange("p (j k u) -> p j k u", j=2, u=2),
                in_=TPX[g][:].rearrange("p j u k -> p j k u"),
            )

        def grouped(step, half):
            if step not in GR:
                GR[step] = gpool.tile([P, 16 * P], BF16, name="gr", tag="gr", align_bytes=64)
            return GR[step][:, half * 8 * P : (half + 1) * 8 * P]

        def quant(step):
            lo = 0 if ok(step + 2) else 2 * P
            hi = 4 * P if ok(step - 2) else 2 * P
            cw = qpool.tile([P, 4 * P], U32, name="cw", tag="cw", align_bytes=64)
            sc = qpool.tile([P, 4 * P], U8, name="sc", tag="sc", align_bytes=64)
            for at in range(lo, hi, 2 * P):
                nc.vector.quantize_mx(
                    out=cw[:, at : at + 2 * P].bitcast(FP8X4), scales=sc[:, at : at + 2 * P],
                    in_=GR[step][:, 4 * at : 4 * at + 8 * P],
                )
            QX[step + 2] = (cw[:, 0 : 2 * P], sc[:, 0 : 2 * P])
            Q1[step - 2] = (cw[:, 2 * P : 4 * P], sc[:, 2 * P : 4 * P])

        def mm(pool, tag, q, wc, ws):
            res = {}
            cw, sc = q
            for j in (1, 0) if tag == "z" else (0, 1):
                acc = pool.tile([P, D], F32, name=tag, tag=tag)
                nc.tensor.matmul_mx(
                    out=acc[:],
                    lhsT=cw[:, j * P : (j + 1) * P].bitcast(FP8X4),
                    lhsT_scale=sc[:, j * P : (j + 1) * P],
                    rhs=wc[:].bitcast(FP8X4),
                    rhs_scale=ws[:],
                    start=True,
                    stop=True,
                )
                res[j] = acc
            return res

        def a1(g, j):
            if j == 0:
                X1[g] = x1pool.tile([P, 2, D], F32, name="x1", tag="x1")
            i = 2 * g + j
            nc.vector.scalar_tensor_tensor(
                out=X1[g][:, j, :], in0=Y[g][j][:], scalar=c32[:, 2 * i : 2 * i + 1],
                in1=x_bf(i), op0=MULT, op1=ADD,
            )

        def cast_views(g, j):
            if g not in X1B:
                X1B[g] = bpool.tile([P, 2 * D], BF16, name="x1b", tag="x1b")
            dst = X1B[g][:, j * D : (j + 1) * D].rearrange("p (u m e) -> p u m e", u=2, e=2)
            src = X1[g][:, j, :].rearrange("p (m u e) -> p u m e", u=2, e=2)
            return dst, src

        def cast_s(g, j):
            dst, src = cast_views(g, j)
            nc.scalar.copy(out=dst, in_=src)

        def cast_v(g, j):
            dst, src = cast_views(g, j)
            nc.vector.tensor_copy(out=dst, in_=src)

        def caster(g):
            return "n" if g == NP - 1 else RULE[g % len(RULE)]

        def t1(g):
            t = ps_t.tile([P, 2, 2, P], F32, name="t1", tag="t1")
            words = X1B[g][:].bitcast(F32)
            plain = caster(g) == "n"
            for j in range(1 if plain else 2):
                for u in range(2):
                    lo = (2 * j + u) * P
                    nc.tensor.transpose(t[:, j, u, :], words[:, lo : lo + P], ident[:])
            T1[g] = [t]
            if plain:
                t2 = ps_t.tile([P, 4, P], F32, name="t1", tag="t1")
                for q in range(4):
                    nc.tensor.transpose(t2[:, q, :], X1[g][:, 1, q::4], ident[:])
                T1[g].append(t2)

        def e1(g):
            g1 = grouped(g + 2, 1)
            if len(T1[g]) == 1:
                nc.scalar.copy(
                    out=g1.bitcast(F32).rearrange("p (j k u) -> p j k u", j=2, u=2),
                    in_=T1[g][0][:].rearrange("p j u k -> p j k u"),
                )
            else:
                nc.scalar.copy(
                    out=g1[:, 0:D].bitcast(F32).rearrange("p (k u) -> p k u", u=2),
                    in_=T1[g][0][:, 0].rearrange("p u k -> p k u"),
                )
                nc.scalar.copy(
                    out=g1[:, D : 2 * D].rearrange("p (k t) -> p k t", t=4),
                    in_=T1[g][1][:].rearrange("p t k -> p k t"),
                )

        def t1_tile(g, j):
            if j == 0:
                t = ps_t.tile([P, 2, P], F32, name="t1", tag="t1")
                words = X1B[g][:].bitcast(F32)
                for u in range(2):
                    nc.tensor.transpose(t[:, u, :], words[:, u * P : (u + 1) * P], ident[:])
            else:
                t = ps_t.tile([P, 4, P], F32, name="t1", tag="t1")
                for q in range(4):
                    nc.tensor.transpose(t[:, q, :], X1[g][:, 1, q::4], ident[:])
            T1[g, j] = t

        def e1_tile(g, j):
            if j == 0:
                nc.scalar.copy(
                    out=grouped(g + 2, 1)[:, 0:D].bitcast(F32).rearrange("p (k u) -> p k u", u=2),
                    in_=T1[g, 0][:].rearrange("p u k -> p k u"),
                )
            else:
                nc.scalar.copy(
                    out=grouped(g + 2, 1)[:, D : 2 * D].rearrange("p (k t) -> p k t", t=4),
                    in_=T1[g, 1][:].rearrange("p t k -> p k t"),
                )

        def q1_tile(g, j):
            if j == 0:
                cw = qpool.tile([P, 2 * P], U32, name="c1", tag="c1", align_bytes=64)
                sc = qpool.tile([P, 2 * P], U8, name="s1", tag="s1", align_bytes=64)
                Q1[g] = (cw, sc)
                Z[g] = {}
            cw, sc = Q1[g]
            nc.vector.quantize_mx(
                out=cw[:, j * P : (j + 1) * P].bitcast(FP8X4),
                scales=sc[:, j * P : (j + 1) * P],
                in_=grouped(g + 2, 1)[:, j * D : (j + 1) * D],
            )

        def z_tile(g, j):
            cw, sc = Q1[g]
            acc = ps_y.tile([P, D], F32, name="y", tag="y")
            nc.tensor.matmul_mx(
                out=acc[:],
                lhsT=cw[:, j * P : (j + 1) * P].bitcast(FP8X4),
                lhsT_scale=sc[:, j * P : (j + 1) * P],
                rhs=w1c[:].bitcast(FP8X4),
                rhs_scale=w1s[:],
                start=True,
                stop=True,
            )
            Z[g][j] = acc

        def a2v(g, j):
            i = 2 * g + j
            nc.vector.scalar_tensor_tensor(
                out=X1[g][:, j, :], in0=Z[g][j][:], scalar=c32[:, 2 * i + 1 : 2 * i + 2],
                in1=X1[g][:, j, :], op0=MULT, op1=ADD,
            )

        def cz(g):
            i = 2 * g + 1
            c, k = where[2 * g]
            t = xs[c][:, k * D : (k + 2) * D].bitcast(F32)
            nc.scalar.activation(
                out=t, in_=Z[g][1][:], func=COPY, scale=c32[:, 2 * i + 1 : 2 * i + 2]
            )
            CZ[g] = t

        def ga(g, h):
            o = grouped(h + 2, 1).bitcast(F32)
            nc.gpsimd.tensor_tensor(out=o, in0=CZ[g], in1=X1[g][:, 1, :], op=ADD)
            return o

        def store_tile(g, j, src):
            i = 2 * g + j
            nc.sync.dma_start(out=o_dram[:, i * D : (i + 1) * D], in_=src)

        def store(g, lo, hi):
            nc.sync.dma_start(
                out=o_dram[:, (2 * g + lo) * D : (2 * g + hi) * D],
                in_=X1[g][:, lo:hi, :].rearrange("p j d -> p (j d)"),
            )

        tx(0)
        ex(0)
        nc.vector.tensor_copy(
            out=w0g[:, 0:W0_SPLIT, :].rearrange("p (c i) t -> p c t i", i=4),
            in_=w0r[:, :, 0:W0_SPLIT].rearrange("p t (c i) -> p c t i", i=4),
        )
        nc.scalar.copy(
            out=w0g[:, W0_SPLIT:D, :].rearrange("p (c i) t -> p c t i", i=4),
            in_=w0r[:, :, W0_SPLIT:D].rearrange("p t (c i) -> p c t i", i=4),
        )
        nc.vector.tensor_copy(out=c32[:], in_=c_bf[:])
        nc.vector.quantize_mx(
            out=w0c[:].bitcast(FP8X4), scales=w0s[:], in_=w0g[:].rearrange("p n t -> p (n t)")
        )

        for it in range(-2, NP):
            if ok(it + 3) and it > 0:
                tx(it + 3)
            if ok(it - 2):
                t1(it - 2)
            if ok(it):
                Y[it] = mm(ps_y, "y", QX[it], w0c, w0s)
            if ok(it - 3):
                Z[it - 3] = mm(ps_z, "z", Q1[it - 3], w1c, w1s)
            if it <= 0:
                tx(it + 3)
            if ok(it - 1):
                cast_s(it - 1, 0)
            if ok(it - 2):
                e1(it - 2)
            if ok(it + 3):
                ex(it + 3)
            if ok(it - 3):
                cz(it - 3)
            if it == -1 or it == 0:
                h = (it + 1) * (D // 2)
                nc.scalar.copy(
                    out=w1g[:, h : h + D // 2, :].rearrange("p (c i) t -> p c t i", i=4),
                    in_=w1r[:, :, h : h + D // 2].rearrange("p t (c i) -> p c t i", i=4),
                )
            if ok(it):
                a1(it, 0)
            if ok(it):
                a1(it, 1)
            quant(it)
            if it == 1:
                nc.vector.quantize_mx(
                    out=w1c[:].bitcast(FP8X4), scales=w1s[:],
                    in_=w1g[:].rearrange("p n t -> p (n t)"),
                )
            if ok(it) and caster(it) == "v":
                cast_v(it, 1)
            if ok(it - 3):
                a2v(it - 3, 0)
            if ok(it - 3):
                store(it - 3, 0, 1)
                store_tile(it - 3, 1, ga(it - 3, it - 2))

        g = NP - 1
        cast_s(g, 0)
        t1(g - 1)
        e1(g - 1)
        Z[g - 2] = mm(ps_z, "z", Q1[g - 2], w1c, w1s)
        t1_tile(g, 0)
        t1_tile(g, 1)
        e1_tile(g, 0)
        e1_tile(g, 1)
        quant(g + 1)
        a2v(g - 2, 1)
        a2v(g - 2, 0)
        store(g - 2, 0, 2)
        Z[g - 1] = mm(ps_z, "z", Q1[g - 1], w1c, w1s)
        q1_tile(g, 0)
        q1_tile(g, 1)
        z_tile(g, 0)
        z_tile(g, 1)
        a2v(g - 1, 1)
        a2v(g - 1, 0)
        store(g - 1, 0, 2)
        a2v(g, 0)
        store(g, 0, 1)
        a2v(g, 1)
        store(g, 1, 2)
